import numpy as np
import ml_dtypes


def mxq(x, axis, fmt="e4m3"):
    dtype, down = {"e4m3": (ml_dtypes.float8_e4m3fn, 7), "e5m2": (ml_dtypes.float8_e5m2, 14)}[fmt]
    v = np.moveaxis(np.asarray(x, np.float32).astype(ml_dtypes.bfloat16).astype(np.float64), axis, -1)
    blocks = v.reshape(v.shape[:-1] + (-1, 32))
    amax = np.abs(blocks).max(-1, keepdims=True)
    byte = np.maximum(np.where(amax > 0, np.frexp(amax)[1] - 1 + 127, 0) - down, 1)
    scale = np.exp2(byte - 127.0)
    codes = (blocks / scale).astype(np.float32).astype(dtype).astype(np.float64)
    return np.moveaxis((codes * scale).reshape(v.shape), -1, axis)


WIDE = False


def mx_kscale(k):
    if not WIDE:
        return np.ones(k)
    levels = np.array([10, -10, 5, -5, 0])
    a = np.random.permutation(np.resize(levels, k // 512 * 4)).reshape(k // 512, 4)
    idx = np.arange(k)
    return np.exp2(a[idx // 512, idx % 128 // 32])


BF16 = ml_dtypes.bfloat16


def bf(x):
    return np.asarray(x, np.float32).astype(BF16)


def f64(x):
    return np.asarray(x).astype(np.float64)


B, N, F_IN, F_OUT, K = 4, 2048, 128, 256, 4


def setup_inputs():
    s = mx_kscale(N)
    r = (s.min() / s)[:, None]
    return {"x": bf(np.random.standard_normal((B, N, F_IN)) * r),
            "L": bf(np.random.standard_normal((N, N)) * 0.7 / np.sqrt(N) * s[None, :] / s[:, None])}


def reference(x, L):
    Lq = mxq(f64(L), 1, "e4m3")
    x1 = Lq @ mxq(f64(x), 1, "e4m3")
    x2 = Lq @ mxq(x1, 1, "e4m3")
    xt2 = 2.0 * x2 - f64(x)
    return x1, x2, xt2

@@ -1,0 +1,220 @@
+from contextlib import ExitStack
+
+import concourse.mybir as mybir
+from concourse.masks import make_identity
+
+F32 = mybir.dt.float32
+BF16 = mybir.dt.bfloat16
+U32 = mybir.dt.uint32
+U8 = mybir.dt.uint8
+FP8X4 = mybir.dt.float8_e4m3fn_x4
+MULT = mybir.AluOpType.mult
+SUB = mybir.AluOpType.subtract
+
+P = 128
+B, N, F = 4, 2048, 128
+NI = N // 256
+NG = N // 512
+FLOPS = 2 * 2 * N * N * B * F
+
+
+def tile_gcncheb_pa_kernel(tc, x, L, out_0, out_1, out_2):
+    nc = tc.nc
+    with ExitStack() as ctx:
+        ctx.enter_context(tc.manual_schedule())
+        keep = ctx.enter_context(tc.tile_pool(name="keep", bufs=1))
+        lgp = ctx.enter_context(tc.tile_pool(name="lgp", bufs=4))
+        xgp = ctx.enter_context(tc.tile_pool(name="xgp", bufs=1))
+        x1gp = ctx.enter_context(tc.tile_pool(name="x1gp", bufs=2))
+        st1p = ctx.enter_context(tc.tile_pool(name="st1p", bufs=4))
+        st2p = ctx.enter_context(tc.tile_pool(name="st2p", bufs=8))
+        st3p = ctx.enter_context(tc.tile_pool(name="st3p", bufs=8))
+        tpp = ctx.enter_context(tc.psum_pool(name="tpp", bufs=4))
+        accp = ctx.enter_context(tc.psum_pool(name="accp", bufs=4))
+
+        ident = keep.tile([P, P], F32, name="ident")
+        make_identity(nc, ident[:])
+
+        lraw = [keep.tile([P, 2, N], BF16, name="lraw%d" % i) for i in range(NI)]
+        xraw = keep.tile([P, B, N], BF16, name="xraw")
+        ltc = keep.tile([P, NI, 2, 512], U32, name="ltc", align_bytes=64)
+        lts = keep.tile([P, NI, 2, 512], U8, name="lts", align_bytes=64)
+        xqc = keep.tile([P, 2, NG, 256], U32, name="xqc", align_bytes=64)
+        xqs = keep.tile([P, 2, NG, 256], U8, name="xqs", align_bytes=64)
+        yqc = keep.tile([P, 2, NG, 256], U32, name="yqc", align_bytes=64)
+        yqs = keep.tile([P, 2, NG, 256], U8, name="yqs", align_bytes=64)
+
+        def load_l(i):
+            nc.sync.dma_start(
+                out=lraw[i][:],
+                in_=L[256 * i : 256 * i + 256, :].rearrange("(p e) b -> p e b", e=2),
+            )
+
+        def load_x(c):
+            nc.sync.dma_start(
+                out=xraw[:, c, :].rearrange("p (i e f) -> p i e f", e=2, f=F),
+                in_=x[c].rearrange("(i p e) f -> p i e f", p=P, e=2),
+            )
+
+        load_l(0)
+        load_x(0)
+        load_x(1)
+        for i in range(1, 7):
+            load_l(i)
+        load_x(2)
+        load_l(7)
+        load_x(3)
+
+        xg_tiles = {}
+
+        def x_regroup(c):
+            h, c2 = divmod(c, 2)
+            if c2 == 0:
+                xg = xgp.tile([P, NG, 2, F, 4], BF16, name="xg", align_bytes=64)
+                xg_tiles[h] = xg
+            nc.vector.tensor_copy(
+                out=xg_tiles[h][:, :, c2, :, :],
+                in_=xraw[:, c, :].rearrange("p (g t f) -> p g f t", t=4, f=F),
+            )
+
+        def x_quant(h):
+            nc.vector.quantize_mx(
+                out=xqc[:, h].rearrange("p g w -> p (g w)").bitcast(FP8X4),
+                scales=xqs[:, h].rearrange("p g w -> p (g w)"),
+                in_=xg_tiles[h][:].rearrange("p g c f t -> p (g c f t)"),
+            )
+
+        lg_tiles = {}
+
+        def transposes(i):
+            for e in range(2):
+                lw = lraw[i][:, e, :].bitcast(F32)
+                lg = lgp.tile([P, N], BF16, name="lg", align_bytes=64)
+                lg_tiles[(i, e)] = lg
+                lgw = lg[:].bitcast(F32).rearrange("p (g c u) -> p g c u", c=P, u=2)
+                for gg in range(2):
+                    tp = tpp.tile([P, 4, P], F32, name="tp")
+                    for s in range(4):
+                        wb = 4 * gg + s
+                        nc.tensor.transpose(tp[:, s, :], lw[:, P * wb : P * wb + P], ident[:])
+                    src = tp[:].rearrange("p (g u) c -> p g c u", u=2)
+                    dst = lgw[:, 2 * gg : 2 * gg + 2, :, :]
+                    if e == 0 and gg == 1:
+                        nc.vector.tensor_copy(out=dst, in_=src)
+                    else:
+                        nc.scalar.copy(out=dst, in_=src)
+
+        def l_quant(i):
+            for e in range(2):
+                nc.vector.quantize_mx(
+                    out=ltc[:, i, e, :].bitcast(FP8X4),
+                    scales=lts[:, i, e, :],
+                    in_=lg_tiles[(i, e)][:],
+                )
+
+        def passes(i, h, rc, rs):
+            acc = accp.tile([P, 2, 256], F32, name="acc")
+            for e in range(2):
+                for g in range(NG):
+                    nc.tensor.matmul_mx(
+                        out=acc[:, e, :],
+                        lhsT=ltc[:, i, e, P * g : P * g + P].bitcast(FP8X4),
+                        lhsT_scale=lts[:, i, e, P * g : P * g + P],
+                        rhs=rc[:, h, g, :].bitcast(FP8X4),
+                        rhs_scale=rs[:, h, g, :],
+                        start=(g == 0),
+                        stop=(g == NG - 1),
+                    )
+            return acc
+
+        def dram_rows(o, i, h):
+            return o[2 * h : 2 * h + 2, 256 * i : 256 * i + 256, :].rearrange(
+                "c (p e) f -> p c e f", e=2
+            )
+
+        st1_tiles = {}
+
+        def hop1_mm(i, h):
+            return passes(i, h, xqc, xqs)
+
+        def hop1_out(i, h, acc):
+            gq, u = divmod(i, 2)
+            if u == 0:
+                st1 = st1p.tile([P, 2, 512], F32, name="st1")
+                st1_tiles[(gq, h)] = st1
+            st1 = st1_tiles[(gq, h)]
+            part = st1[:, :, 256 * u : 256 * u + 256].rearrange("p c (e f) -> p c e f", e=2)
+            nc.scalar.copy(out=part, in_=acc[:].rearrange("p e (c f) -> p c e f", c=2))
+            nc.sync.dma_start(out=dram_rows(out_0, i, h), in_=part)
+
+        def hop1_quant(gq, h):
+            x1g = x1gp.tile([P, 2, F, 4], BF16, name="x1g", align_bytes=64)
+            nc.vector.tensor_copy(
+                out=x1g[:],
+                in_=st1_tiles[(gq, h)][:].rearrange("p c (t f) -> p c f t", t=4),
+            )
+            nc.vector.quantize_mx(
+                out=yqc[:, h, gq, :].bitcast(FP8X4),
+                scales=yqs[:, h, gq, :],
+                in_=x1g[:].rearrange("p c f t -> p (c f t)"),
+            )
+
+        def hop2(i, h):
+            acc = passes(i, h, yqc, yqs)
+            st2 = st2p.tile([P, 2, 256], F32, name="st2")
+            st3 = st3p.tile([P, 2, 256], F32, name="st3")
+            nc.scalar.copy(
+                out=st2[:].rearrange("p c (e f) -> p c e f", e=2),
+                in_=acc[:].rearrange("p e (c f) -> p c e f", c=2),
+            )
+            nc.sync.dma_start(
+                out=dram_rows(out_1, i, h), in_=st2[:].rearrange("p c (e f) -> p c e f", e=2)
+            )
+            nc.vector.scalar_tensor_tensor(
+                out=st3[:],
+                in0=st2[:],
+                scalar=2.0,
+                in1=xraw[:, 2 * h : 2 * h + 2, 256 * i : 256 * i + 256],
+                op0=MULT,
+                op1=SUB,
+            )
+            nc.sync.dma_start(
+                out=dram_rows(out_2, i, h), in_=st3[:].rearrange("p c (e f) -> p c e f", e=2)
+            )
+
+        transposes(0)
+        l_quant(0)
+        x_regroup(0)
+        x_regroup(1)
+        x_quant(0)
+        for i in range(NI):
+            if i + 1 < NI:
+                transposes(i + 1)
+            acc = hop1_mm(i, 0)
+            if i % 2 == 0 and i > 0:
+                hop1_quant(i // 2 - 1, 0)
+            if i + 1 < NI:
+                l_quant(i + 1)
+            if i == 6:
+                x_regroup(2)
+            hop1_out(i, 0, acc)
+        x_regroup(3)
+        x_quant(1)
+        hop1_quant(3, 0)
+
+        def hop1_b(i):
+            acc = hop1_mm(i, 1)
+            hop1_out(i, 1, acc)
+            if i % 2 == 1:
+                hop1_quant(i // 2, 1)
+
+        for i in range(3):
+            hop1_b(i)
+        for j in range(5):
+            hop2(j, 0)
+            hop1_b(j + 3)
+        for j in range(5, NI):
+            hop2(j, 0)
+
+        for j in range(NI):
+            hop2(j, 1)

@@ -24,13 +24,15 @@ def tile_gcncheb_pa_kernel(tc, x, L, out_0, out_1, out_2):
         ctx.enter_context(tc.manual_schedule())
         keep = ctx.enter_context(tc.tile_pool(name="keep", bufs=1))
         lgp = ctx.enter_context(tc.tile_pool(name="lgp", bufs=4))
-        xgp = ctx.enter_context(tc.tile_pool(name="xgp", bufs=1))
+        xgp = ctx.enter_context(tc.tile_pool(name="xgp", bufs=2))
         x1gp = ctx.enter_context(tc.tile_pool(name="x1gp", bufs=2))
         st1p = ctx.enter_context(tc.tile_pool(name="st1p", bufs=4))
         st2p = ctx.enter_context(tc.tile_pool(name="st2p", bufs=8))
         st3p = ctx.enter_context(tc.tile_pool(name="st3p", bufs=8))
-        tpp = ctx.enter_context(tc.psum_pool(name="tpp", bufs=4))
-        accp = ctx.enter_context(tc.psum_pool(name="accp", bufs=4))
+        psum = ctx.enter_context(tc.psum_pool(name="psum", bufs=1))
+
+        def bank(k, shape):
+            return psum.tile(shape, F32, name="bank%d" % k, tag="bank%d" % k)
 
         ident = keep.tile([P, P], F32, name="ident")
         make_identity(nc, ident[:])
@@ -59,11 +61,17 @@ def tile_gcncheb_pa_kernel(tc, x, L, out_0, out_1, out_2):
         load_l(0)
         load_x(0)
         load_x(1)
-        for i in range(1, 7):
+        for i in range(1, NI):
             load_l(i)
         load_x(2)
-        load_l(7)
         load_x(3)
+
+        def warm(c, k):
+            w = bank(k, [P, 512])
+            for r in range(3):
+                nc.tensor.matmul(
+                    out=w[:], lhsT=xraw[:, c, 0:P], rhs=xraw[:, c, 0:512], start=True, stop=True
+                )
 
         xg_tiles = {}
 
@@ -86,20 +94,20 @@ def tile_gcncheb_pa_kernel(tc, x, L, out_0, out_1, out_2):
 
         lg_tiles = {}
 
-        def transposes(i):
+        def transposes(i, on_vector):
             for e in range(2):
                 lw = lraw[i][:, e, :].bitcast(F32)
                 lg = lgp.tile([P, N], BF16, name="lg", align_bytes=64)
                 lg_tiles[(i, e)] = lg
                 lgw = lg[:].bitcast(F32).rearrange("p (g c u) -> p g c u", c=P, u=2)
                 for gg in range(2):
-                    tp = tpp.tile([P, 4, P], F32, name="tp")
+                    tp = bank(2 * e + gg, [P, 4, P])
                     for s in range(4):
                         wb = 4 * gg + s
                         nc.tensor.transpose(tp[:, s, :], lw[:, P * wb : P * wb + P], ident[:])
                     src = tp[:].rearrange("p (g u) c -> p g c u", u=2)
                     dst = lgw[:, 2 * gg : 2 * gg + 2, :, :]
-                    if e == 0 and gg == 1:
+                    if 2 * e + gg in on_vector:
                         nc.vector.tensor_copy(out=dst, in_=src)
                     else:
                         nc.scalar.copy(out=dst, in_=src)
@@ -112,19 +120,22 @@ def tile_gcncheb_pa_kernel(tc, x, L, out_0, out_1, out_2):
                     in_=lg_tiles[(i, e)][:],
                 )
 
-        def passes(i, h, rc, rs):
-            acc = accp.tile([P, 2, 256], F32, name="acc")
+        def one_pass(out, i, e, g, h, rc, rs):
+            nc.tensor.matmul_mx(
+                out=out,
+                lhsT=ltc[:, i, e, P * g : P * g + P].bitcast(FP8X4),
+                lhsT_scale=lts[:, i, e, P * g : P * g + P],
+                rhs=rc[:, h, g, :].bitcast(FP8X4),
+                rhs_scale=rs[:, h, g, :],
+                start=(g == 0),
+                stop=(g == NG - 1),
+            )
+
+        def passes(k, i, h, rc, rs):
+            acc = bank(k, [P, 2, 256])
             for e in range(2):
                 for g in range(NG):
-                    nc.tensor.matmul_mx(
-                        out=acc[:, e, :],
-                        lhsT=ltc[:, i, e, P * g : P * g + P].bitcast(FP8X4),
-                        lhsT_scale=lts[:, i, e, P * g : P * g + P],
-                        rhs=rc[:, h, g, :].bitcast(FP8X4),
-                        rhs_scale=rs[:, h, g, :],
-                        start=(g == 0),
-                        stop=(g == NG - 1),
-                    )
+                    one_pass(acc[:, e, :], i, e, g, h, rc, rs)
             return acc
 
         def dram_rows(o, i, h):
@@ -132,18 +143,17 @@ def tile_gcncheb_pa_kernel(tc, x, L, out_0, out_1, out_2):
                 "c (p e) f -> p c e f", e=2
             )
 
-        st1_tiles = {}
+        def split_ef(ap):
+            return ap.rearrange("p c (e f) -> p c e f", e=2)
 
-        def hop1_mm(i, h):
-            return passes(i, h, xqc, xqs)
+        st1_tiles = {}
 
         def hop1_out(i, h, acc):
             gq, u = divmod(i, 2)
             if u == 0:
                 st1 = st1p.tile([P, 2, 512], F32, name="st1")
                 st1_tiles[(gq, h)] = st1
-            st1 = st1_tiles[(gq, h)]
-            part = st1[:, :, 256 * u : 256 * u + 256].rearrange("p c (e f) -> p c e f", e=2)
+            part = split_ef(st1_tiles[(gq, h)][:, :, 256 * u : 256 * u + 256])
             nc.scalar.copy(out=part, in_=acc[:].rearrange("p e (c f) -> p c e f", c=2))
             nc.sync.dma_start(out=dram_rows(out_0, i, h), in_=part)
 
@@ -159,17 +169,23 @@ def tile_gcncheb_pa_kernel(tc, x, L, out_0, out_1, out_2):
                 in_=x1g[:].rearrange("p c f t -> p (c f t)"),
             )
 
-        def hop2(i, h):
-            acc = passes(i, h, yqc, yqs)
+        def hop2_x2(i, h, accs):
             st2 = st2p.tile([P, 2, 256], F32, name="st2")
+            if len(accs) == 1:
+                nc.scalar.copy(
+                    out=split_ef(st2[:]), in_=accs[0][:].rearrange("p e (c f) -> p c e f", c=2)
+                )
+            else:
+                for e in range(2):
+                    nc.scalar.copy(
+                        out=split_ef(st2[:])[:, :, e, :],
+                        in_=accs[e][:].rearrange("p (c f) -> p c f", c=2),
+                    )
+            nc.sync.dma_start(out=dram_rows(out_1, i, h), in_=split_ef(st2[:]))
+            return st2
+
+        def hop2_xt2(i, h, st2):
             st3 = st3p.tile([P, 2, 256], F32, name="st3")
-            nc.scalar.copy(
-                out=st2[:].rearrange("p c (e f) -> p c e f", e=2),
-                in_=acc[:].rearrange("p e (c f) -> p c e f", c=2),
-            )
-            nc.sync.dma_start(
-                out=dram_rows(out_1, i, h), in_=st2[:].rearrange("p c (e f) -> p c e f", e=2)
-            )
             nc.vector.scalar_tensor_tensor(
                 out=st3[:],
                 in0=st2[:],
@@ -178,42 +194,73 @@ def tile_gcncheb_pa_kernel(tc, x, L, out_0, out_1, out_2):
                 op0=MULT,
                 op1=SUB,
             )
-            nc.sync.dma_start(
-                out=dram_rows(out_2, i, h), in_=st3[:].rearrange("p c (e f) -> p c e f", e=2)
-            )
+            nc.sync.dma_start(out=dram_rows(out_2, i, h), in_=split_ef(st3[:]))
 
-        transposes(0)
-        l_quant(0)
+        transposes(0, ())
+        warm(0, 4)
+        warm(1, 5)
         x_regroup(0)
+        l_quant(0)
         x_regroup(1)
         x_quant(0)
         for i in range(NI):
             if i + 1 < NI:
-                transposes(i + 1)
-            acc = hop1_mm(i, 0)
-            if i % 2 == 0 and i > 0:
-                hop1_quant(i // 2 - 1, 0)
-            if i + 1 < NI:
+                transposes(i + 1, (1, 3) if i + 1 == NI - 1 else (1,))
+            acc = passes(4 + i % 4, i, 0, xqc, xqs)
+            if i == NI - 2:
                 l_quant(i + 1)
-            if i == 6:
-                x_regroup(2)
+                hop1_quant(i // 2 - 1, 0)
+            else:
+                if i % 2 == 0 and i > 0:
+                    hop1_quant(i // 2 - 1, 0)
+                if i + 1 < NI:
+                    l_quant(i + 1)
             hop1_out(i, 0, acc)
+        x_regroup(2)
+
+        n_open = 4
+        opened = {}
+        for j in range(n_open):
+            opened[j] = []
+            for e in range(2):
+                acc = bank(2 * j + e, [P, 256])
+                for g in range(NG - 1):
+                    one_pass(acc[:], j, e, g, 0, yqc, yqs)
+                opened[j].append(acc)
+        hop1_quant(3, 0)
         x_regroup(3)
         x_quant(1)
-        hop1_quant(3, 0)
+        st2_open = {}
+        for j in range(n_open):
+            for e in range(2):
+                one_pass(opened[j][e][:], j, e, NG - 1, 0, yqc, yqs)
+            st2_open[j] = hop2_x2(j, 0, opened[j])
+        for j in range(n_open):
+            hop2_xt2(j, 0, st2_open[j])
+
+        rot = [0]
+
+        def next_bank():
+            k = rot[0] % 8
+            rot[0] += 1
+            return k
 
         def hop1_b(i):
-            acc = hop1_mm(i, 1)
+            acc = passes(next_bank(), i, 1, xqc, xqs)
             hop1_out(i, 1, acc)
             if i % 2 == 1:
                 hop1_quant(i // 2, 1)
 
-        for i in range(3):
+        def hop2(i, h):
+            acc = passes(next_bank(), i, h, yqc, yqs)
+            st2 = hop2_x2(i, h, [acc])
+            hop2_xt2(i, h, st2)
+
+        for i in range(NI):
             hop1_b(i)
-        for j in range(5):
-            hop2(j, 0)
-            hop1_b(j + 3)
-        for j in range(5, NI):
+            if i == NI - 2:
+                hop2(n_open, 0)
+        for j in range(n_open + 1, NI):
             hop2(j, 0)
 
         for j in range(NI):

@@ -216,9 +216,8 @@ def tile_gcncheb_pa_kernel(tc, x, L, out_0, out_1, out_2):
                 if i + 1 < NI:
                     l_quant(i + 1)
             hop1_out(i, 0, acc)
-        x_regroup(2)
 
-        n_open = 4
+        n_open = 3
         opened = {}
         for j in range(n_open):
             opened[j] = []
@@ -228,17 +227,18 @@ def tile_gcncheb_pa_kernel(tc, x, L, out_0, out_1, out_2):
                     one_pass(acc[:], j, e, g, 0, yqc, yqs)
                 opened[j].append(acc)
         hop1_quant(3, 0)
-        x_regroup(3)
-        x_quant(1)
+        x_regroup(2)
         st2_open = {}
         for j in range(n_open):
             for e in range(2):
                 one_pass(opened[j][e][:], j, e, NG - 1, 0, yqc, yqs)
             st2_open[j] = hop2_x2(j, 0, opened[j])
+        x_regroup(3)
+        x_quant(1)
         for j in range(n_open):
             hop2_xt2(j, 0, st2_open[j])
 
-        rot = [0]
+        rot = [2 * n_open]
 
         def next_bank():
             k = rot[0] % 8
@@ -256,12 +256,14 @@ def tile_gcncheb_pa_kernel(tc, x, L, out_0, out_1, out_2):
             st2 = hop2_x2(i, h, [acc])
             hop2_xt2(i, h, st2)
 
+        hop2(3, 0)
+        hop2(4, 0)
         for i in range(NI):
             hop1_b(i)
             if i == NI - 2:
-                hop2(n_open, 0)
-        for j in range(n_open + 1, NI):
-            hop2(j, 0)
+                hop2(5, 0)
+        hop2(6, 0)
+        hop2(7, 0)
 
         for j in range(NI):
             hop2(j, 1)

@@ -66,13 +66,6 @@ def tile_gcncheb_pa_kernel(tc, x, L, out_0, out_1, out_2):
         load_x(2)
         load_x(3)
 
-        def warm(c, k):
-            w = bank(k, [P, 512])
-            for r in range(3):
-                nc.tensor.matmul(
-                    out=w[:], lhsT=xraw[:, c, 0:P], rhs=xraw[:, c, 0:512], start=True, stop=True
-                )
-
         xg_tiles = {}
 
         def x_regroup(c):
@@ -197,8 +190,6 @@ def tile_gcncheb_pa_kernel(tc, x, L, out_0, out_1, out_2):
             nc.sync.dma_start(out=dram_rows(out_2, i, h), in_=split_ef(st3[:]))
 
         transposes(0, ())
-        warm(0, 4)
-        warm(1, 5)
         x_regroup(0)
         l_quant(0)
         x_regroup(1)

@@ -21,7 +21,6 @@ FLOPS = 2 * 2 * N * N * B * F
 def tile_gcncheb_pa_kernel(tc, x, L, out_0, out_1, out_2):
     nc = tc.nc
     with ExitStack() as ctx:
-        ctx.enter_context(tc.manual_schedule())
         keep = ctx.enter_context(tc.tile_pool(name="keep", bufs=1))
         lgp = ctx.enter_context(tc.tile_pool(name="lgp", bufs=4))
         xgp = ctx.enter_context(tc.tile_pool(name="xgp", bufs=2))
@@ -65,6 +64,13 @@ def tile_gcncheb_pa_kernel(tc, x, L, out_0, out_1, out_2):
             load_l(i)
         load_x(2)
         load_x(3)
+
+        def warm(c, k):
+            w = bank(k, [P, 512])
+            for r in range(3):
+                nc.tensor.matmul(
+                    out=w[:], lhsT=xraw[:, c, 0:P], rhs=xraw[:, c, 0:512], start=True, stop=True
+                )
 
         xg_tiles = {}
 
@@ -190,6 +196,8 @@ def tile_gcncheb_pa_kernel(tc, x, L, out_0, out_1, out_2):
             nc.sync.dma_start(out=dram_rows(out_2, i, h), in_=split_ef(st3[:]))
 
         transposes(0, ())
+        warm(0, 4)
+        warm(1, 5)
         x_regroup(0)
         l_quant(0)
         x_regroup(1)

@@ -21,6 +21,7 @@ FLOPS = 2 * 2 * N * N * B * F
 def tile_gcncheb_pa_kernel(tc, x, L, out_0, out_1, out_2):
     nc = tc.nc
     with ExitStack() as ctx:
+        ctx.enter_context(tc.manual_schedule())
         keep = ctx.enter_context(tc.tile_pool(name="keep", bufs=1))
         lgp = ctx.enter_context(tc.tile_pool(name="lgp", bufs=4))
         xgp = ctx.enter_context(tc.tile_pool(name="xgp", bufs=2))
@@ -111,13 +112,12 @@ def tile_gcncheb_pa_kernel(tc, x, L, out_0, out_1, out_2):
                     else:
                         nc.scalar.copy(out=dst, in_=src)
 
-        def l_quant(i):
-            for e in range(2):
-                nc.vector.quantize_mx(
-                    out=ltc[:, i, e, :].bitcast(FP8X4),
-                    scales=lts[:, i, e, :],
-                    in_=lg_tiles[(i, e)][:],
-                )
+        def l_quant(i, e):
+            nc.vector.quantize_mx(
+                out=ltc[:, i, e, :].bitcast(FP8X4),
+                scales=lts[:, i, e, :],
+                in_=lg_tiles[(i, e)][:],
+            )
 
         def one_pass(out, i, e, g, h, rc, rs):
             nc.tensor.matmul_mx(
@@ -156,17 +156,23 @@ def tile_gcncheb_pa_kernel(tc, x, L, out_0, out_1, out_2):
             nc.scalar.copy(out=part, in_=acc[:].rearrange("p e (c f) -> p c e f", c=2))
             nc.sync.dma_start(out=dram_rows(out_0, i, h), in_=part)
 
-        def hop1_quant(gq, h):
+        def hop1_regroup(gq, h):
             x1g = x1gp.tile([P, 2, F, 4], BF16, name="x1g", align_bytes=64)
             nc.vector.tensor_copy(
                 out=x1g[:],
                 in_=st1_tiles[(gq, h)][:].rearrange("p c (t f) -> p c f t", t=4),
             )
+            return x1g
+
+        def hop1_codes(gq, h, x1g):
             nc.vector.quantize_mx(
                 out=yqc[:, h, gq, :].bitcast(FP8X4),
                 scales=yqs[:, h, gq, :],
                 in_=x1g[:].rearrange("p c f t -> p (c f t)"),
             )
+
+        def hop1_quant(gq, h):
+            hop1_codes(gq, h, hop1_regroup(gq, h))
 
         def hop2_x2(i, h, accs):
             st2 = st2p.tile([P, 2, 256], F32, name="st2")
@@ -199,21 +205,23 @@ def tile_gcncheb_pa_kernel(tc, x, L, out_0, out_1, out_2):
         warm(0, 4)
         warm(1, 5)
         x_regroup(0)
-        l_quant(0)
+        l_quant(0, 0)
         x_regroup(1)
+        l_quant(0, 1)
         x_quant(0)
         for i in range(NI):
             if i + 1 < NI:
-                transposes(i + 1, (1, 3) if i + 1 == NI - 1 else (1,))
+                transposes(i + 1, (1, 2) if i + 1 == NI - 1 else (2,))
             acc = passes(4 + i % 4, i, 0, xqc, xqs)
-            if i == NI - 2:
-                l_quant(i + 1)
-                hop1_quant(i // 2 - 1, 0)
-            else:
-                if i % 2 == 0 and i > 0:
-                    hop1_quant(i // 2 - 1, 0)
-                if i + 1 < NI:
-                    l_quant(i + 1)
+            ready = i % 2 == 0 and i > 0
+            if i + 1 < NI:
+                l_quant(i + 1, 0)
+            if ready:
+                x1g = hop1_regroup(i // 2 - 1, 0)
+            if i + 1 < NI:
+                l_quant(i + 1, 1)
+            if ready:
+                hop1_codes(i // 2 - 1, 0, x1g)
             hop1_out(i, 0, acc)
 
         n_open = 3

from contextlib import ExitStack

import concourse.mybir as mybir
from concourse.masks import make_identity

F32 = mybir.dt.float32
BF16 = mybir.dt.bfloat16
U32 = mybir.dt.uint32
U8 = mybir.dt.uint8
FP8X4 = mybir.dt.float8_e4m3fn_x4
MULT = mybir.AluOpType.mult
SUB = mybir.AluOpType.subtract

P = 128
B, N, F = 4, 2048, 128
NI = N // 256
NG = N // 512
FLOPS = 2 * 2 * N * N * B * F


def tile_gcncheb_pa_kernel(tc, x, L, out_0, out_1, out_2):
    nc = tc.nc
    with ExitStack() as ctx:
        ctx.enter_context(tc.manual_schedule())
        keep = ctx.enter_context(tc.tile_pool(name="keep", bufs=1))
        lgp = ctx.enter_context(tc.tile_pool(name="lgp", bufs=4))
        xgp = ctx.enter_context(tc.tile_pool(name="xgp", bufs=2))
        x1gp = ctx.enter_context(tc.tile_pool(name="x1gp", bufs=2))
        st1p = ctx.enter_context(tc.tile_pool(name="st1p", bufs=4))
        st2p = ctx.enter_context(tc.tile_pool(name="st2p", bufs=8))
        st3p = ctx.enter_context(tc.tile_pool(name="st3p", bufs=8))
        psum = ctx.enter_context(tc.psum_pool(name="psum", bufs=1))

        def bank(k, shape):
            return psum.tile(shape, F32, name="bank%d" % k, tag="bank%d" % k)

        ident = keep.tile([P, P], F32, name="ident")
        make_identity(nc, ident[:])

        lraw = [keep.tile([P, 2, N], BF16, name="lraw%d" % i) for i in range(NI)]
        xraw = keep.tile([P, B, N], BF16, name="xraw")
        ltc = keep.tile([P, NI, 2, 512], U32, name="ltc", align_bytes=64)
        lts = keep.tile([P, NI, 2, 512], U8, name="lts", align_bytes=64)
        xqc = keep.tile([P, 2, NG, 256], U32, name="xqc", align_bytes=64)
        xqs = keep.tile([P, 2, NG, 256], U8, name="xqs", align_bytes=64)
        yqc = keep.tile([P, 2, NG, 256], U32, name="yqc", align_bytes=64)
        yqs = keep.tile([P, 2, NG, 256], U8, name="yqs", align_bytes=64)

        def load_l(i):
            nc.sync.dma_start(
                out=lraw[i][:],
                in_=L[256 * i : 256 * i + 256, :].rearrange("(p e) b -> p e b", e=2),
            )

        def load_x(c):
            nc.sync.dma_start(
                out=xraw[:, c, :].rearrange("p (i e f) -> p i e f", e=2, f=F),
                in_=x[c].rearrange("(i p e) f -> p i e f", p=P, e=2),
            )

        load_l(0)
        load_x(0)
        load_x(1)
        for i in range(1, NI):
            load_l(i)
        load_x(2)
        load_x(3)

        def warm(c, k):
            w = bank(k, [P, 512])
            for r in range(3):
                nc.tensor.matmul(
                    out=w[:], lhsT=xraw[:, c, 0:P], rhs=xraw[:, c, 0:512], start=True, stop=True
                )

        xg_tiles = {}

        def x_regroup(c):
            h, c2 = divmod(c, 2)
            if c2 == 0:
                xg = xgp.tile([P, NG, 2, F, 4], BF16, name="xg", align_bytes=64)
                xg_tiles[h] = xg
            nc.vector.tensor_copy(
                out=xg_tiles[h][:, :, c2, :, :],
                in_=xraw[:, c, :].rearrange("p (g t f) -> p g f t", t=4, f=F),
            )

        def x_quant(h):
            nc.vector.quantize_mx(
                out=xqc[:, h].rearrange("p g w -> p (g w)").bitcast(FP8X4),
                scales=xqs[:, h].rearrange("p g w -> p (g w)"),
                in_=xg_tiles[h][:].rearrange("p g c f t -> p (g c f t)"),
            )

        lg_tiles = {}

        def transposes(i, on_vector):
            for e in range(2):
                lw = lraw[i][:, e, :].bitcast(F32)
                lg = lgp.tile([P, N], BF16, name="lg", align_bytes=64)
                lg_tiles[(i, e)] = lg
                lgw = lg[:].bitcast(F32).rearrange("p (g c u) -> p g c u", c=P, u=2)
                for gg in range(2):
                    tp = bank(2 * e + gg, [P, 4, P])
                    for s in range(4):
                        wb = 4 * gg + s
                        nc.tensor.transpose(tp[:, s, :], lw[:, P * wb : P * wb + P], ident[:])
                    src = tp[:].rearrange("p (g u) c -> p g c u", u=2)
                    dst = lgw[:, 2 * gg : 2 * gg + 2, :, :]
                    if 2 * e + gg in on_vector:
                        nc.vector.tensor_copy(out=dst, in_=src)
                    else:
                        nc.scalar.copy(out=dst, in_=src)

        def l_quant(i, e):
            nc.vector.quantize_mx(
                out=ltc[:, i, e, :].bitcast(FP8X4),
                scales=lts[:, i, e, :],
                in_=lg_tiles[(i, e)][:],
            )

        def one_pass(out, i, e, g, h, rc, rs):
            nc.tensor.matmul_mx(
                out=out,
                lhsT=ltc[:, i, e, P * g : P * g + P].bitcast(FP8X4),
                lhsT_scale=lts[:, i, e, P * g : P * g + P],
                rhs=rc[:, h, g, :].bitcast(FP8X4),
                rhs_scale=rs[:, h, g, :],
                start=(g == 0),
                stop=(g == NG - 1),
            )

        def passes(k, i, h, rc, rs):
            acc = bank(k, [P, 2, 256])
            for e in range(2):
                for g in range(NG):
                    one_pass(acc[:, e, :], i, e, g, h, rc, rs)
            return acc

        def dram_rows(o, i, h):
            return o[2 * h : 2 * h + 2, 256 * i : 256 * i + 256, :].rearrange(
                "c (p e) f -> p c e f", e=2
            )

        def split_ef(ap):
            return ap.rearrange("p c (e f) -> p c e f", e=2)

        st1_tiles = {}

        def hop1_out(i, h, acc):
            gq, u = divmod(i, 2)
            if u == 0:
                st1 = st1p.tile([P, 2, 512], F32, name="st1")
                st1_tiles[(gq, h)] = st1
            part = split_ef(st1_tiles[(gq, h)][:, :, 256 * u : 256 * u + 256])
            nc.scalar.copy(out=part, in_=acc[:].rearrange("p e (c f) -> p c e f", c=2))
            nc.sync.dma_start(out=dram_rows(out_0, i, h), in_=part)

        def hop1_regroup(gq, h):
            x1g = x1gp.tile([P, 2, F, 4], BF16, name="x1g", align_bytes=64)
            nc.vector.tensor_copy(
                out=x1g[:],
                in_=st1_tiles[(gq, h)][:].rearrange("p c (t f) -> p c f t", t=4),
            )
            return x1g

        def hop1_codes(gq, h, x1g):
            nc.vector.quantize_mx(
                out=yqc[:, h, gq, :].bitcast(FP8X4),
                scales=yqs[:, h, gq, :],
                in_=x1g[:].rearrange("p c f t -> p (c f t)"),
            )

        def hop1_quant(gq, h):
            hop1_codes(gq, h, hop1_regroup(gq, h))

        def hop2_x2(i, h, accs):
            st2 = st2p.tile([P, 2, 256], F32, name="st2")
            if len(accs) == 1:
                nc.scalar.copy(
                    out=split_ef(st2[:]), in_=accs[0][:].rearrange("p e (c f) -> p c e f", c=2)
                )
            else:
                for e in range(2):
                    nc.scalar.copy(
                        out=split_ef(st2[:])[:, :, e, :],
                        in_=accs[e][:].rearrange("p (c f) -> p c f", c=2),
                    )
            nc.sync.dma_start(out=dram_rows(out_1, i, h), in_=split_ef(st2[:]))
            return st2

        def hop2_xt2(i, h, st2):
            st3 = st3p.tile([P, 2, 256], F32, name="st3")
            nc.vector.scalar_tensor_tensor(
                out=st3[:],
                in0=st2[:],
                scalar=2.0,
                in1=xraw[:, 2 * h : 2 * h + 2, 256 * i : 256 * i + 256],
                op0=MULT,
                op1=SUB,
            )
            nc.sync.dma_start(out=dram_rows(out_2, i, h), in_=split_ef(st3[:]))

        transposes(0, ())
        warm(0, 4)
        warm(1, 5)
        x_regroup(0)
        l_quant(0, 0)
        x_regroup(1)
        l_quant(0, 1)
        x_quant(0)
        for i in range(NI):
            if i + 1 < NI:
                transposes(i + 1, (1, 2) if i + 1 == NI - 1 else (2,))
            acc = passes(4 + i % 4, i, 0, xqc, xqs)
            ready = i % 2 == 0 and i > 0
            if i + 1 < NI:
                l_quant(i + 1, 0)
            if ready:
                x1g = hop1_regroup(i // 2 - 1, 0)
            if i + 1 < NI:
                l_quant(i + 1, 1)
            if ready:
                hop1_codes(i // 2 - 1, 0, x1g)
            hop1_out(i, 0, acc)

        n_open = 3
        opened = {}
        for j in range(n_open):
            opened[j] = []
            for e in range(2):
                acc = bank(2 * j + e, [P, 256])
                for g in range(NG - 1):
                    one_pass(acc[:], j, e, g, 0, yqc, yqs)
                opened[j].append(acc)
        hop1_quant(3, 0)
        x_regroup(2)
        st2_open = {}
        for j in range(n_open):
            for e in range(2):
                one_pass(opened[j][e][:], j, e, NG - 1, 0, yqc, yqs)
            st2_open[j] = hop2_x2(j, 0, opened[j])
        x_regroup(3)
        x_quant(1)
        for j in range(n_open):
            hop2_xt2(j, 0, st2_open[j])

        rot = [2 * n_open]

        def next_bank():
            k = rot[0] % 8
            rot[0] += 1
            return k

        def hop1_b(i):
            acc = passes(next_bank(), i, 1, xqc, xqs)
            hop1_out(i, 1, acc)
            if i % 2 == 1:
                hop1_quant(i // 2, 1)

        def hop2(i, h):
            acc = passes(next_bank(), i, h, yqc, yqs)
            st2 = hop2_x2(i, h, [acc])
            hop2_xt2(i, h, st2)

        hop2(3, 0)
        hop2(4, 0)
        for i in range(NI):
            hop1_b(i)
            if i == NI - 2:
                hop2(5, 0)
        hop2(6, 0)
        hop2(7, 0)

        for j in range(NI):
            hop2(j, 1)
